import numpy as np
import ml_dtypes


def mxq(x, axis, fmt="e4m3"):
    dtype, down = {"e4m3": (ml_dtypes.float8_e4m3fn, 7), "e5m2": (ml_dtypes.float8_e5m2, 14)}[fmt]
    v = np.moveaxis(np.asarray(x, np.float32).astype(ml_dtypes.bfloat16).astype(np.float64), axis, -1)
    blocks = v.reshape(v.shape[:-1] + (-1, 32))
    amax = np.abs(blocks).max(-1, keepdims=True)
    byte = np.maximum(np.where(amax > 0, np.frexp(amax)[1] - 1 + 127, 0) - down, 1)
    scale = np.exp2(byte - 127.0)
    codes = (blocks / scale).astype(np.float32).astype(dtype).astype(np.float64)
    return np.moveaxis((codes * scale).reshape(v.shape), -1, axis)


WIDE = False


def mx_kscale(k):
    if not WIDE:
        return np.ones(k)
    levels = np.array([10, -10, 5, -5, 0])
    a = np.random.permutation(np.resize(levels, k // 512 * 4)).reshape(k // 512, 4)
    idx = np.arange(k)
    return np.exp2(a[idx // 512, idx % 128 // 32])


BF16 = ml_dtypes.bfloat16


def bf(x):
    return np.asarray(x, np.float32).astype(BF16)


def f64(x):
    return np.asarray(x).astype(np.float64)


E2M1 = np.array([0.0, 0.5, 1.0, 1.5, 2.0, 3.0, 4.0, 6.0, -0.0, -0.5, -1.0, -1.5, -2.0, -3.0, -4.0, -6.0])


def pack_weight(w, fmt):
    k, n = w.shape
    w = f64(bf(w)).reshape(k // 32, 32, n)
    amax = np.abs(w).max(1)
    if fmt == "e4m3":
        byte = np.frexp(amax)[1] - 1 + 127 - 7
    else:
        mant, ex = np.frexp(amax / 6.0)
        byte = np.where(mant > 0.5, ex, ex - 1) + 127
    byte = np.clip(np.where(amax > 0, byte, 1), 1, 254)
    scaled = (w * np.exp2(127.0 - byte)[:, None, :]).reshape(k, n).astype(np.float32)
    by_word = np.ascontiguousarray(scaled.reshape(k // 512, 128, 4, n).transpose(0, 1, 3, 2))
    if fmt == "e4m3":
        words = by_word.astype(ml_dtypes.float8_e4m3fn).view(np.uint8)
    else:
        c = by_word.astype(ml_dtypes.float4_e2m1fn).view(np.uint8) & 0xF
        words = c[..., 0::2] | (c[..., 1::2] << 4)
    return np.ascontiguousarray(words), np.ascontiguousarray(byte.astype(np.uint8).reshape(k // 512, 16, n))


def unpack_weight(words, scales, fmt):
    g, p, n, _ = words.shape
    if fmt == "e4m3":
        vals = np.ascontiguousarray(words).view(ml_dtypes.float8_e4m3fn).astype(np.float64)
    else:
        nib = np.empty((g, p, n, 4), np.uint8)
        nib[..., 0::2] = words & 0xF
        nib[..., 1::2] = words >> 4
        vals = E2M1[nib]
    vals = vals * np.repeat(np.exp2(scales.astype(np.float64) - 127.0), 8, axis=1)[..., None]
    return vals.transpose(0, 1, 3, 2).reshape(g * 512, n)


B, H, E, V = 512, 1024, 1024, 4096
FMT = "e4m3"


def sigmoid(v):
    return 1.0 / (1.0 + np.exp(-v))


def draw_w(k, n, div):
    return pack_weight(np.random.standard_normal((k, n)) / np.sqrt(k) / div[:, None], FMT)


def setup_inputs():
    s, t = mx_kscale(E), mx_kscale(H)
    one = np.ones(H)
    inputs = {
        "input_data": bf(np.random.standard_normal((B, E)) * s),
        "previous_hidden_state": bf(np.random.standard_normal((B, H)) * t),
        "previous_c_state": bf(np.random.standard_normal((B, H))),
    }
    for name, k, div in (
        ("w_forget", H, t),
        ("w_input", H, t),
        ("w_c_dash", H, t),
        ("w_forget_c", H, one),
        ("w_input_c", H, one),
        ("w_ip_f", E, s),
        ("w_ip_i", E, s),
        ("w_ip_c_dash", E, s),
    ):
        words, scales = draw_w(k, H, div)
        inputs[name + "_words"] = words
        inputs[name + "_scales"] = scales
    return inputs


def reference(input_data, previous_hidden_state, previous_c_state,
              w_forget_words, w_forget_scales, w_input_words, w_input_scales,
              w_c_dash_words, w_c_dash_scales, w_forget_c_words, w_forget_c_scales,
              w_input_c_words, w_input_c_scales, w_ip_f_words, w_ip_f_scales,
              w_ip_i_words, w_ip_i_scales, w_ip_c_dash_words, w_ip_c_dash_scales):
    c = f64(previous_c_state)
    xq = mxq(f64(input_data), 1, "e4m3")
    hq = mxq(f64(previous_hidden_state), 1, "e4m3")
    cq = mxq(c, 1, "e4m3")
    zf = (xq @ unpack_weight(w_ip_f_words, w_ip_f_scales, FMT)) + (hq @ unpack_weight(w_forget_words, w_forget_scales, FMT))
    zi = (xq @ unpack_weight(w_ip_i_words, w_ip_i_scales, FMT)) + (hq @ unpack_weight(w_input_words, w_input_scales, FMT))
    zc = (xq @ unpack_weight(w_ip_c_dash_words, w_ip_c_dash_scales, FMT)) + (hq @ unpack_weight(w_c_dash_words, w_c_dash_scales, FMT))
    ft = sigmoid(zf + (cq @ unpack_weight(w_forget_c_words, w_forget_c_scales, FMT)))
    it = sigmoid(zi + (cq @ unpack_weight(w_input_c_words, w_input_c_scales, FMT)))
    ct_dash = np.tanh(zc)
    return ft * c + it * ct_dash

@@ -1,0 +1,220 @@
+from contextlib import ExitStack
+
+import concourse.mybir as mybir
+from concourse.masks import make_identity
+
+FP8X4 = mybir.dt.float8_e4m3fn_x4
+BF16 = mybir.dt.bfloat16
+F32 = mybir.dt.float32
+I32 = mybir.dt.int32
+U32 = mybir.dt.uint32
+U8 = mybir.dt.uint8
+ACT = mybir.ActivationFunctionType
+
+P = 128
+PACK = 4
+K_PASS = P * PACK
+PAIR = 2
+N_TILE = 512
+
+BATCH = 512
+K = 1024
+N = 1024
+ROW_BLOCKS = BATCH // P
+K_GROUPS = K // K_PASS
+HALVES = N // N_TILE
+QUADRANTS = 4
+
+FLOPS = 8 * 2 * BATCH * K * N
+
+X, H, C = 0, 1, 2
+CANDIDATE = ((X, 0), (H, 1))
+INPUT_GATE = ((X, 2), (H, 3), (C, 4))
+FORGET_GATE = ((X, 5), (H, 6), (C, 7))
+
+
+def tile_lstm_peephole_build_pa_kernel(
+    tc,
+    input_data,
+    previous_hidden_state,
+    previous_c_state,
+    w_forget_words,
+    w_forget_scales,
+    w_input_words,
+    w_input_scales,
+    w_c_dash_words,
+    w_c_dash_scales,
+    w_forget_c_words,
+    w_forget_c_scales,
+    w_input_c_words,
+    w_input_c_scales,
+    w_ip_f_words,
+    w_ip_f_scales,
+    w_ip_i_words,
+    w_ip_i_scales,
+    w_ip_c_dash_words,
+    w_ip_c_dash_scales,
+    out,
+):
+    nc = tc.nc
+    activations = (input_data, previous_hidden_state, previous_c_state)
+    weights = (
+        (w_ip_c_dash_words, w_ip_c_dash_scales),
+        (w_c_dash_words, w_c_dash_scales),
+        (w_ip_i_words, w_ip_i_scales),
+        (w_input_words, w_input_scales),
+        (w_input_c_words, w_input_c_scales),
+        (w_ip_f_words, w_ip_f_scales),
+        (w_forget_words, w_forget_scales),
+        (w_forget_c_words, w_forget_c_scales),
+    )
+
+    with ExitStack() as ctx:
+        keep = ctx.enter_context(tc.tile_pool(name="keep", bufs=1))
+        stage = ctx.enter_context(tc.tile_pool(name="stage", bufs=ROW_BLOCKS))
+        work = ctx.enter_context(tc.tile_pool(name="work", bufs=ROW_BLOCKS))
+        psum = ctx.enter_context(tc.psum_pool(name="psum", bufs=8))
+        ctx.enter_context(tc.manual_schedule())
+
+        identity = keep.tile([P, P], F32)
+        rows = [keep.tile([P, ROW_BLOCKS, K], BF16, name="rows%d" % a) for a in range(3)]
+        act_codes = [
+            keep.tile([P, ROW_BLOCKS, K_GROUPS * P], U32, name="act_codes%d" % a, align_bytes=64) for a in range(3)
+        ]
+        act_scales = [
+            keep.tile([P, ROW_BLOCKS, K_GROUPS * P], U8, name="act_scales%d" % a, align_bytes=64) for a in range(3)
+        ]
+        w_codes = [
+            keep.tile([P, HALVES, K_GROUPS, N_TILE], U32, name="w_codes%d" % w, align_bytes=64)
+            for w in range(len(weights))
+        ]
+        w_scales = keep.tile([P, len(weights) // 2, N], U8, align_bytes=64)
+        new_part = keep.tile([P, ROW_BLOCKS, HALVES, N_TILE], F32)
+
+        make_identity(nc, identity[:])
+        nc.vector.memset(w_scales[:].bitcast(I32), 0)
+
+        def load_rows(a):
+            for rb in range(ROW_BLOCKS):
+                nc.sync.dma_start(out=rows[a][:, rb, :], in_=activations[a][rb * P : (rb + 1) * P, :])
+
+        def load_codes(w, half):
+            source = weights[w][0].rearrange("g p n t -> p g (n t)")
+            nc.sync.dma_start(
+                out=w_codes[w][:, half, :, :].bitcast(I32),
+                in_=source[:, :, half * N_TILE * PACK : (half + 1) * N_TILE * PACK].bitcast(I32),
+            )
+
+        def load_scales(w):
+            for quadrant in range(QUADRANTS):
+                low = 32 * quadrant + 8 * (w % 2)
+                nc.sync.dma_start(
+                    out=w_scales[low : low + 8, w // 2, :].bitcast(I32),
+                    in_=weights[w][1][:, 4 * quadrant : 4 * quadrant + 4, :].bitcast(I32),
+                )
+
+        load_rows(X)
+        load_scales(0)
+        load_scales(1)
+        load_codes(0, 0)
+        load_rows(H)
+        load_codes(1, 0)
+        load_codes(0, 1)
+        load_codes(1, 1)
+        load_rows(C)
+        for w in (2, 3, 4, 5):
+            load_scales(w)
+        for half in range(HALVES):
+            for w in (2, 3, 4):
+                load_codes(w, half)
+        for w in (6, 7):
+            load_scales(w)
+        for half in range(HALVES):
+            for w in (5, 6, 7):
+                load_codes(w, half)
+
+        def quantise_activation(a):
+            grouped_tiles = []
+            for rb in range(ROW_BLOCKS):
+                words = rows[a][:, rb, :].bitcast(F32)
+                sorted_words = stage.tile([P, K_GROUPS, PAIR, P], F32)
+                nc.vector.tensor_copy(
+                    out=sorted_words[:], in_=words.rearrange("r (g p u) -> r g u p", g=K_GROUPS, u=PAIR)
+                )
+                turned = psum.tile([P, K_GROUPS, PAIR, P], F32, tag="bank")
+                for g in range(K_GROUPS):
+                    for u in range(PAIR):
+                        nc.tensor.transpose(turned[:, g, u, :], sorted_words[:, g, u, :], identity[:])
+                grouped = stage.tile([P, K_GROUPS * P * PACK], BF16, align_bytes=64)
+                nc.scalar.copy(
+                    out=grouped[:].bitcast(F32).rearrange("p (g r u) -> p g r u", g=K_GROUPS, u=PAIR),
+                    in_=turned[:].rearrange("p g u r -> p g r u"),
+                )
+                grouped_tiles.append(grouped)
+            for rb in range(ROW_BLOCKS):
+                nc.vector.quantize_mx(
+                    out=act_codes[a][:, rb, :].bitcast(FP8X4),
+                    scales=act_scales[a][:, rb, :],
+                    in_=grouped_tiles[rb][:],
+                )
+
+        def new_banks():
+            return [psum.tile([P, N_TILE], F32, name="sum%d" % rb, tag="bank") for rb in range(ROW_BLOCKS)]
+
+        def multiply(bank, term, rb, half, first, last):
+            a, w = term
+            for g in range(K_GROUPS):
+                plane_start = 8 * (w % 2) + 4 * g
+                nc.tensor.matmul_mx(
+                    out=bank[:],
+                    lhsT=act_codes[a][:, rb, g * P : (g + 1) * P].bitcast(FP8X4),
+                    lhsT_scale=act_scales[a][:, rb, g * P : (g + 1) * P],
+                    rhs=w_codes[w][:, half, g, :].bitcast(FP8X4),
+                    rhs_scale=w_scales[plane_start:P, w // 2, half * N_TILE : (half + 1) * N_TILE],
+                    start=(first and g == 0),
+                    stop=(last and g == K_GROUPS - 1),
+                )
+
+        def finish_candidate(bank, rb, half):
+            nc.scalar.activation(out=new_part[:, rb, half, :], in_=bank[:], func=ACT.Tanh)
+
+        def finish_input_gate(bank, rb, half):
+            gate = work.tile([P, N_TILE], F32)
+            nc.scalar.activation(out=gate[:], in_=bank[:], func=ACT.Sigmoid)
+            nc.vector.tensor_mul(out=new_part[:, rb, half, :], in0=gate[:], in1=new_part[:, rb, half, :])
+
+        def finish_forget_gate(bank, rb, half):
+            gate = work.tile([P, N_TILE], F32)
+            nc.scalar.activation(out=gate[:], in_=bank[:], func=ACT.Sigmoid)
+            columns = slice(half * N_TILE, (half + 1) * N_TILE)
+            nc.vector.tensor_mul(out=gate[:], in0=gate[:], in1=rows[C][:, rb, columns])
+            nc.vector.tensor_add(out=gate[:], in0=gate[:], in1=new_part[:, rb, half, :])
+            nc.sync.dma_start(out=out[rb * P : (rb + 1) * P, columns], in_=gate[:])
+
+        def term_by_term(banks, terms, half, finish, first_term):
+            for i in range(first_term, len(terms)):
+                last = i == len(terms) - 1
+                for rb in range(ROW_BLOCKS):
+                    multiply(banks[rb], terms[i], rb, half, first=(i == 0), last=last)
+                    if last:
+                        finish(banks[rb], rb, half)
+
+        def block_by_block(terms, half, finish):
+            banks = new_banks()
+            for rb in range(ROW_BLOCKS):
+                for i in range(len(terms)):
+                    multiply(banks[rb], terms[i], rb, half, first=(i == 0), last=(i == len(terms) - 1))
+                finish(banks[rb], rb, half)
+
+        quantise_activation(X)
+        banks = new_banks()
+        for rb in range(ROW_BLOCKS):
+            multiply(banks[rb], CANDIDATE[0], rb, 0, first=True, last=False)
+        quantise_activation(H)
+        term_by_term(banks, CANDIDATE, 0, finish_candidate, first_term=1)
+        term_by_term(new_banks(), CANDIDATE, 1, finish_candidate, first_term=0)
+        quantise_activation(C)
+        for half in range(HALVES):
+            term_by_term(new_banks(), INPUT_GATE, half, finish_input_gate, first_term=0)
+        term_by_term(new_banks(), FORGET_GATE, 0, finish_forget_gate, first_term=0)
+        block_by_block(FORGET_GATE, 1, finish_forget_gate)

@@ -15,15 +15,17 @@ P = 128
 PACK = 4
 K_PASS = P * PACK
 PAIR = 2
-N_TILE = 512
+BANK = 512
+PSUM_BANKS = 8
 
 BATCH = 512
 K = 1024
 N = 1024
 ROW_BLOCKS = BATCH // P
 K_GROUPS = K // K_PASS
-HALVES = N // N_TILE
+HALVES = N // BANK
 QUADRANTS = 4
+LAST_WIDTH = 256
 
 FLOPS = 8 * 2 * BATCH * K * N
 
@@ -72,11 +74,12 @@ def tile_lstm_peephole_build_pa_kernel(
     with ExitStack() as ctx:
         keep = ctx.enter_context(tc.tile_pool(name="keep", bufs=1))
         stage = ctx.enter_context(tc.tile_pool(name="stage", bufs=ROW_BLOCKS))
-        work = ctx.enter_context(tc.tile_pool(name="work", bufs=ROW_BLOCKS))
-        psum = ctx.enter_context(tc.psum_pool(name="psum", bufs=8))
+        work = ctx.enter_context(tc.tile_pool(name="work", bufs=2 * ROW_BLOCKS))
+        psum = ctx.enter_context(tc.psum_pool(name="psum", bufs=PSUM_BANKS))
         ctx.enter_context(tc.manual_schedule())
 
         identity = keep.tile([P, P], F32)
+        table_warmer = keep.tile([P, 1], F32)
         rows = [keep.tile([P, ROW_BLOCKS, K], BF16, name="rows%d" % a) for a in range(3)]
         act_codes = [
             keep.tile([P, ROW_BLOCKS, K_GROUPS * P], U32, name="act_codes%d" % a, align_bytes=64) for a in range(3)
@@ -85,14 +88,17 @@ def tile_lstm_peephole_build_pa_kernel(
             keep.tile([P, ROW_BLOCKS, K_GROUPS * P], U8, name="act_scales%d" % a, align_bytes=64) for a in range(3)
         ]
         w_codes = [
-            keep.tile([P, HALVES, K_GROUPS, N_TILE], U32, name="w_codes%d" % w, align_bytes=64)
+            keep.tile([P, HALVES, K_GROUPS, BANK], U32, name="w_codes%d" % w, align_bytes=64)
             for w in range(len(weights))
         ]
-        w_scales = keep.tile([P, len(weights) // 2, N], U8, align_bytes=64)
-        new_part = keep.tile([P, ROW_BLOCKS, HALVES, N_TILE], F32)
+        w_scales = [keep.tile([P, N], U8, name="w_scales%d" % w, align_bytes=64) for w in range(len(weights))]
+        new_part = keep.tile([P, ROW_BLOCKS, N], F32)
 
         make_identity(nc, identity[:])
-        nc.vector.memset(w_scales[:].bitcast(I32), 0)
+        nc.vector.memset(table_warmer[:], 0.0)
+        nc.scalar.activation(out=table_warmer[:], in_=table_warmer[:], func=ACT.Sigmoid)
+        for w in range(len(weights)):
+            nc.vector.memset(w_scales[w][:].bitcast(I32), 0)
 
         def load_rows(a):
             for rb in range(ROW_BLOCKS):
@@ -102,36 +108,28 @@ def tile_lstm_peephole_build_pa_kernel(
             source = weights[w][0].rearrange("g p n t -> p g (n t)")
             nc.sync.dma_start(
                 out=w_codes[w][:, half, :, :].bitcast(I32),
-                in_=source[:, :, half * N_TILE * PACK : (half + 1) * N_TILE * PACK].bitcast(I32),
+                in_=source[:, :, half * BANK * PACK : (half + 1) * BANK * PACK].bitcast(I32),
             )
 
-        def load_scales(w):
+        def load_scales(w, queue, view):
             for quadrant in range(QUADRANTS):
-                low = 32 * quadrant + 8 * (w % 2)
-                nc.sync.dma_start(
-                    out=w_scales[low : low + 8, w // 2, :].bitcast(I32),
-                    in_=weights[w][1][:, 4 * quadrant : 4 * quadrant + 4, :].bitcast(I32),
+                queue.dma_start(
+                    out=w_scales[w][32 * quadrant : 32 * quadrant + 4 * K_GROUPS, :].bitcast(view),
+                    in_=weights[w][1][:, 4 * quadrant : 4 * quadrant + 4, :].bitcast(view),
                 )
 
-        load_rows(X)
-        load_scales(0)
-        load_scales(1)
-        load_codes(0, 0)
-        load_rows(H)
-        load_codes(1, 0)
-        load_codes(0, 1)
-        load_codes(1, 1)
-        load_rows(C)
-        for w in (2, 3, 4, 5):
-            load_scales(w)
-        for half in range(HALVES):
-            for w in (2, 3, 4):
-                load_codes(w, half)
-        for w in (6, 7):
-            load_scales(w)
-        for half in range(HALVES):
-            for w in (5, 6, 7):
-                load_codes(w, half)
+        rows_loaded = set()
+        for terms in (CANDIDATE, INPUT_GATE, FORGET_GATE):
+            for half in range(HALVES):
+                for a, w in terms:
+                    if a not in rows_loaded:
+                        load_rows(a)
+                        rows_loaded.add(a)
+                    if w < len(CANDIDATE) and half == 0:
+                        load_scales(w, nc.sync, I32)
+                    load_codes(w, half)
+        for w in range(len(CANDIDATE), len(weights)):
+            load_scales(w, nc.gpsimd, F32)
 
         def quantise_activation(a):
             grouped_tiles = []
@@ -158,63 +156,64 @@ def tile_lstm_peephole_build_pa_kernel(
                     in_=grouped_tiles[rb][:],
                 )
 
-        def new_banks():
-            return [psum.tile([P, N_TILE], F32, name="sum%d" % rb, tag="bank") for rb in range(ROW_BLOCKS)]
-
-        def multiply(bank, term, rb, half, first, last):
+        def multiply(bank, term, rb, column, width, first, last):
             a, w = term
+            half, inner = divmod(column, BANK)
             for g in range(K_GROUPS):
-                plane_start = 8 * (w % 2) + 4 * g
                 nc.tensor.matmul_mx(
                     out=bank[:],
                     lhsT=act_codes[a][:, rb, g * P : (g + 1) * P].bitcast(FP8X4),
                     lhsT_scale=act_scales[a][:, rb, g * P : (g + 1) * P],
-                    rhs=w_codes[w][:, half, g, :].bitcast(FP8X4),
-                    rhs_scale=w_scales[plane_start:P, w // 2, half * N_TILE : (half + 1) * N_TILE],
+                    rhs=w_codes[w][:, half, g, inner : inner + width].bitcast(FP8X4),
+                    rhs_scale=w_scales[w][4 * g : P, column : column + width],
                     start=(first and g == 0),
                     stop=(last and g == K_GROUPS - 1),
                 )
 
-        def finish_candidate(bank, rb, half):
-            nc.scalar.activation(out=new_part[:, rb, half, :], in_=bank[:], func=ACT.Tanh)
+        def finish_candidate(bank, rb, column, width):
+            nc.scalar.activation(out=new_part[:, rb, column : column + width], in_=bank[:], func=ACT.Tanh)
 
-        def finish_input_gate(bank, rb, half):
-            gate = work.tile([P, N_TILE], F32)
+        def finish_input_gate(bank, rb, column, width):
+            gate = work.tile([P, width], F32)
             nc.scalar.activation(out=gate[:], in_=bank[:], func=ACT.Sigmoid)
-            nc.vector.tensor_mul(out=new_part[:, rb, half, :], in0=gate[:], in1=new_part[:, rb, half, :])
+            product = new_part[:, rb, column : column + width]
+            nc.vector.tensor_mul(out=product, in0=gate[:], in1=product)
 
-        def finish_forget_gate(bank, rb, half):
-            gate = work.tile([P, N_TILE], F32)
+        def finish_forget_gate(bank, rb, column, width):
+            gate = work.tile([P, width], F32)
             nc.scalar.activation(out=gate[:], in_=bank[:], func=ACT.Sigmoid)
-            columns = slice(half * N_TILE, (half + 1) * N_TILE)
-            nc.vector.tensor_mul(out=gate[:], in0=gate[:], in1=rows[C][:, rb, columns])
-            nc.vector.tensor_add(out=gate[:], in0=gate[:], in1=new_part[:, rb, half, :])
-            nc.sync.dma_start(out=out[rb * P : (rb + 1) * P, columns], in_=gate[:])
+            nc.vector.tensor_mul(out=gate[:], in0=gate[:], in1=rows[C][:, rb, column : column + width])
+            nc.vector.tensor_add(out=gate[:], in0=gate[:], in1=new_part[:, rb, column : column + width])
+            nc.sync.dma_start(out=out[rb * P : (rb + 1) * P, column : column + width], in_=gate[:])
 
-        def term_by_term(banks, terms, half, finish, first_term):
-            for i in range(first_term, len(terms)):
+        quantised = set()
+
+        def term_by_term(terms, half, finish):
+            banks = []
+            for i in range(len(terms)):
+                a = terms[i][0]
+                if a not in quantised:
+                    quantise_activation(a)
+                    quantised.add(a)
                 last = i == len(terms) - 1
                 for rb in range(ROW_BLOCKS):
-                    multiply(banks[rb], terms[i], rb, half, first=(i == 0), last=last)
+                    if i == 0:
+                        banks.append(psum.tile([P, BANK], F32, name="sums", tag="bank"))
+                    multiply(banks[rb], terms[i], rb, half * BANK, BANK, first=(i == 0), last=last)
                     if last:
-                        finish(banks[rb], rb, half)
+                        finish(banks[rb], rb, half * BANK, BANK)
 
-        def block_by_block(terms, half, finish):
-            banks = new_banks()
+        def bank_by_bank(terms, half, finish, width):
             for rb in range(ROW_BLOCKS):
-                for i in range(len(terms)):
-                    multiply(banks[rb], terms[i], rb, half, first=(i == 0), last=(i == len(terms) - 1))
-                finish(banks[rb], rb, half)
+                for column in range(half * BANK, (half + 1) * BANK, width):
+                    sums = psum.tile([P, width], F32, tag="bank")
+                    for i in range(len(terms)):
+                        multiply(sums, terms[i], rb, column, width, first=(i == 0), last=(i == len(terms) - 1))
+                    finish(sums, rb, column, width)
 
-        quantise_activation(X)
-        banks = new_banks()
-        for rb in range(ROW_BLOCKS):
-            multiply(banks[rb], CANDIDATE[0], rb, 0, first=True, last=False)
-        quantise_activation(H)
-        term_by_term(banks, CANDIDATE, 0, finish_candidate, first_term=1)
-        term_by_term(new_banks(), CANDIDATE, 1, finish_candidate, first_term=0)
-        quantise_activation(C)
         for half in range(HALVES):
-            term_by_term(new_banks(), INPUT_GATE, half, finish_input_gate, first_term=0)
-        term_by_term(new_banks(), FORGET_GATE, 0, finish_forget_gate, first_term=0)
-        block_by_block(FORGET_GATE, 1, finish_forget_gate)
+            term_by_term(CANDIDATE, half, finish_candidate)
+        for half in range(HALVES):
+            term_by_term(INPUT_GATE, half, finish_input_gate)
+        bank_by_bank(FORGET_GATE, 0, finish_forget_gate, BANK)
+        bank_by_bank(FORGET_GATE, 1, finish_forget_gate, LAST_WIDTH)

@@ -111,11 +111,11 @@ def tile_lstm_peephole_build_pa_kernel(
                 in_=source[:, :, half * BANK * PACK : (half + 1) * BANK * PACK].bitcast(I32),
             )
 
-        def load_scales(w, queue, view):
+        def load_scales(w):
             for quadrant in range(QUADRANTS):
-                queue.dma_start(
-                    out=w_scales[w][32 * quadrant : 32 * quadrant + 4 * K_GROUPS, :].bitcast(view),
-                    in_=weights[w][1][:, 4 * quadrant : 4 * quadrant + 4, :].bitcast(view),
+                nc.sync.dma_start(
+                    out=w_scales[w][32 * quadrant : 32 * quadrant + 4 * K_GROUPS, :].bitcast(I32),
+                    in_=weights[w][1][:, 4 * quadrant : 4 * quadrant + 4, :].bitcast(I32),
                 )
 
         rows_loaded = set()
@@ -125,11 +125,9 @@ def tile_lstm_peephole_build_pa_kernel(
                     if a not in rows_loaded:
                         load_rows(a)
                         rows_loaded.add(a)
-                    if w < len(CANDIDATE) and half == 0:
-                        load_scales(w, nc.sync, I32)
+                    if half == 0:
+                        load_scales(w)
                     load_codes(w, half)
-        for w in range(len(CANDIDATE), len(weights)):
-            load_scales(w, nc.gpsimd, F32)
 
         def quantise_activation(a):
             grouped_tiles = []

@@ -25,7 +25,8 @@ ROW_BLOCKS = BATCH // P
 K_GROUPS = K // K_PASS
 HALVES = N // BANK
 QUADRANTS = 4
-LAST_WIDTH = 256
+LATE_WIDTHS = (256, 256)
+LAST_WIDTHS = (256, 128, 128)
 
 FLOPS = 8 * 2 * BATCH * K * N
 
@@ -177,12 +178,20 @@ def tile_lstm_peephole_build_pa_kernel(
             product = new_part[:, rb, column : column + width]
             nc.vector.tensor_mul(out=product, in0=gate[:], in1=product)
 
+        waiting_sums = []
+
+        def add_and_store():
+            gate, rb, column, width = waiting_sums.pop(0)
+            nc.vector.tensor_add(out=gate[:], in0=gate[:], in1=new_part[:, rb, column : column + width])
+            nc.sync.dma_start(out=out[rb * P : (rb + 1) * P, column : column + width], in_=gate[:])
+
         def finish_forget_gate(bank, rb, column, width):
             gate = work.tile([P, width], F32)
             nc.scalar.activation(out=gate[:], in_=bank[:], func=ACT.Sigmoid)
             nc.vector.tensor_mul(out=gate[:], in0=gate[:], in1=rows[C][:, rb, column : column + width])
-            nc.vector.tensor_add(out=gate[:], in0=gate[:], in1=new_part[:, rb, column : column + width])
-            nc.sync.dma_start(out=out[rb * P : (rb + 1) * P, column : column + width], in_=gate[:])
+            waiting_sums.append((gate, rb, column, width))
+            if len(waiting_sums) > 1:
+                add_and_store()
 
         quantised = set()
 
@@ -201,17 +210,20 @@ def tile_lstm_peephole_build_pa_kernel(
                     if last:
                         finish(banks[rb], rb, half * BANK, BANK)
 
-        def bank_by_bank(terms, half, finish, width):
+        def bank_by_bank(terms, half, finish, widths, last_widths):
             for rb in range(ROW_BLOCKS):
-                for column in range(half * BANK, (half + 1) * BANK, width):
+                column = half * BANK
+                for width in last_widths if rb == ROW_BLOCKS - 1 else widths:
                     sums = psum.tile([P, width], F32, tag="bank")
                     for i in range(len(terms)):
                         multiply(sums, terms[i], rb, column, width, first=(i == 0), last=(i == len(terms) - 1))
                     finish(sums, rb, column, width)
+                    column += width
 
         for half in range(HALVES):
             term_by_term(CANDIDATE, half, finish_candidate)
         for half in range(HALVES):
             term_by_term(INPUT_GATE, half, finish_input_gate)
-        bank_by_bank(FORGET_GATE, 0, finish_forget_gate, BANK)
-        bank_by_bank(FORGET_GATE, 1, finish_forget_gate, LAST_WIDTH)
+        bank_by_bank(FORGET_GATE, 0, finish_forget_gate, (BANK,), (BANK,))
+        bank_by_bank(FORGET_GATE, 1, finish_forget_gate, LATE_WIDTHS, LAST_WIDTHS)
+        add_and_store()

@@ -24,6 +24,7 @@ N = 1024
 ROW_BLOCKS = BATCH // P
 K_GROUPS = K // K_PASS
 HALVES = N // BANK
+ROWS_DMA = 2
 QUADRANTS = 4
 LATE_WIDTHS = (256, 256)
 LAST_WIDTHS = (256, 128, 128)
@@ -102,8 +103,11 @@ def tile_lstm_peephole_build_pa_kernel(
             nc.vector.memset(w_scales[w][:].bitcast(I32), 0)
 
         def load_rows(a):
-            for rb in range(ROW_BLOCKS):
-                nc.sync.dma_start(out=rows[a][:, rb, :], in_=activations[a][rb * P : (rb + 1) * P, :])
+            for first in range(0, ROW_BLOCKS, ROWS_DMA):
+                nc.sync.dma_start(
+                    out=rows[a][:, first : first + ROWS_DMA, :],
+                    in_=activations[a][first * P : (first + ROWS_DMA) * P, :].rearrange("(b p) k -> p b k", p=P),
+                )
 
         def load_codes(w, half):
             source = weights[w][0].rearrange("g p n t -> p g (n t)")

@@ -24,6 +24,7 @@ N = 1024
 ROW_BLOCKS = BATCH // P
 K_GROUPS = K // K_PASS
 HALVES = N // BANK
+WARM_MATMULS = 7
 ROWS_DMA = 2
 QUADRANTS = 4
 LATE_WIDTHS = (256, 256)
@@ -96,6 +97,11 @@ def tile_lstm_peephole_build_pa_kernel(
         w_scales = [keep.tile([P, N], U8, name="w_scales%d" % w, align_bytes=64) for w in range(len(weights))]
         new_part = keep.tile([P, ROW_BLOCKS, N], F32)
 
+        warm_zeros = keep.tile([P, BANK], BF16)
+        nc.vector.memset(warm_zeros[:], 0.0)
+        warm_bank = psum.tile([P, BANK], F32, tag="bank")
+        for i in range(WARM_MATMULS):
+            nc.tensor.matmul(out=warm_bank[:], lhsT=warm_zeros[:, 0:P], rhs=warm_zeros[:], start=True, stop=True)
         make_identity(nc, identity[:])
         nc.vector.memset(table_warmer[:], 0.0)
         nc.scalar.activation(out=table_warmer[:], in_=table_warmer[:], func=ACT.Sigmoid)

@@ -17,6 +17,8 @@ K_PASS = P * PACK
 PAIR = 2
 BANK = 512
 PSUM_BANKS = 8
+LOW_BANKS = (0, 1, 2, 3)
+HIGH_BANKS = (4, 5, 6, 7)
 
 BATCH = 512
 K = 1024
@@ -78,8 +80,11 @@ def tile_lstm_peephole_build_pa_kernel(
         keep = ctx.enter_context(tc.tile_pool(name="keep", bufs=1))
         stage = ctx.enter_context(tc.tile_pool(name="stage", bufs=ROW_BLOCKS))
         work = ctx.enter_context(tc.tile_pool(name="work", bufs=2 * ROW_BLOCKS))
-        psum = ctx.enter_context(tc.psum_pool(name="psum", bufs=PSUM_BANKS))
+        psum = ctx.enter_context(tc.psum_pool(name="psum", bufs=1))
         ctx.enter_context(tc.manual_schedule())
+
+        def bank_tile(index, shape):
+            return psum.tile(shape, F32, name="bank%d" % index, tag="bank%d" % index)
 
         identity = keep.tile([P, P], F32)
         table_warmer = keep.tile([P, 1], F32)
@@ -99,7 +104,7 @@ def tile_lstm_peephole_build_pa_kernel(
 
         warm_zeros = keep.tile([P, BANK], BF16)
         nc.vector.memset(warm_zeros[:], 0.0)
-        warm_bank = psum.tile([P, BANK], F32, tag="bank")
+        warm_bank = bank_tile(HIGH_BANKS[0], [P, BANK])
         for i in range(WARM_MATMULS):
             nc.tensor.matmul(out=warm_bank[:], lhsT=warm_zeros[:, 0:P], rhs=warm_zeros[:], start=True, stop=True)
         make_identity(nc, identity[:])
@@ -115,12 +120,13 @@ def tile_lstm_peephole_build_pa_kernel(
                     in_=activations[a][first * P : (first + ROWS_DMA) * P, :].rearrange("(b p) k -> p b k", p=P),
                 )
 
-        def load_codes(w, half):
+        def load_codes(w, half, groups_dma=K_GROUPS):
             source = weights[w][0].rearrange("g p n t -> p g (n t)")
-            nc.sync.dma_start(
-                out=w_codes[w][:, half, :, :].bitcast(I32),
-                in_=source[:, :, half * BANK * PACK : (half + 1) * BANK * PACK].bitcast(I32),
-            )
+            for g in range(0, K_GROUPS, groups_dma):
+                nc.sync.dma_start(
+                    out=w_codes[w][:, half, g : g + groups_dma, :].bitcast(I32),
+                    in_=source[:, g : g + groups_dma, half * BANK * PACK : (half + 1) * BANK * PACK].bitcast(I32),
+                )
 
         def load_scales(w):
             for quadrant in range(QUADRANTS):
@@ -129,8 +135,16 @@ def tile_lstm_peephole_build_pa_kernel(
                     in_=weights[w][1][:, 4 * quadrant : 4 * quadrant + 4, :].bitcast(I32),
                 )
 
-        rows_loaded = set()
-        for terms in (CANDIDATE, INPUT_GATE, FORGET_GATE):
+        load_rows(X)
+        load_scales(CANDIDATE[0][1])
+        load_codes(CANDIDATE[0][1], 0, groups_dma=1)
+        load_rows(H)
+        load_codes(CANDIDATE[0][1], 1)
+        load_scales(CANDIDATE[1][1])
+        load_codes(CANDIDATE[1][1], 0)
+        load_codes(CANDIDATE[1][1], 1)
+        rows_loaded = set((X, H))
+        for terms in (INPUT_GATE, FORGET_GATE):
             for half in range(HALVES):
                 for a, w in terms:
                     if a not in rows_loaded:
@@ -148,7 +162,7 @@ def tile_lstm_peephole_build_pa_kernel(
                 nc.vector.tensor_copy(
                     out=sorted_words[:], in_=words.rearrange("r (g p u) -> r g u p", g=K_GROUPS, u=PAIR)
                 )
-                turned = psum.tile([P, K_GROUPS, PAIR, P], F32, tag="bank")
+                turned = bank_tile(LOW_BANKS[rb], [P, K_GROUPS, PAIR, P])
                 for g in range(K_GROUPS):
                     for u in range(PAIR):
                         nc.tensor.transpose(turned[:, g, u, :], sorted_words[:, g, u, :], identity[:])
@@ -165,19 +179,22 @@ def tile_lstm_peephole_build_pa_kernel(
                     in_=grouped_tiles[rb][:],
                 )
 
-        def multiply(bank, term, rb, column, width, first, last):
+        def one_pass(bank, term, rb, g, column, width, first, last):
             a, w = term
             half, inner = divmod(column, BANK)
+            nc.tensor.matmul_mx(
+                out=bank[:],
+                lhsT=act_codes[a][:, rb, g * P : (g + 1) * P].bitcast(FP8X4),
+                lhsT_scale=act_scales[a][:, rb, g * P : (g + 1) * P],
+                rhs=w_codes[w][:, half, g, inner : inner + width].bitcast(FP8X4),
+                rhs_scale=w_scales[w][4 * g : P, column : column + width],
+                start=(first and g == 0),
+                stop=(last and g == K_GROUPS - 1),
+            )
+
+        def multiply(bank, term, rb, column, width, first, last):
             for g in range(K_GROUPS):
-                nc.tensor.matmul_mx(
-                    out=bank[:],
-                    lhsT=act_codes[a][:, rb, g * P : (g + 1) * P].bitcast(FP8X4),
-                    lhsT_scale=act_scales[a][:, rb, g * P : (g + 1) * P],
-                    rhs=w_codes[w][:, half, g, inner : inner + width].bitcast(FP8X4),
-                    rhs_scale=w_scales[w][4 * g : P, column : column + width],
-                    start=(first and g == 0),
-                    stop=(last and g == K_GROUPS - 1),
-                )
+                one_pass(bank, term, rb, g, column, width, first, last)
 
         def finish_candidate(bank, rb, column, width):
             nc.scalar.activation(out=new_part[:, rb, column : column + width], in_=bank[:], func=ACT.Tanh)
@@ -203,37 +220,48 @@ def tile_lstm_peephole_build_pa_kernel(
             if len(waiting_sums) > 1:
                 add_and_store()
 
-        quantised = set()
+        def open_banks(indices):
+            return [bank_tile(index, [P, BANK]) for index in indices]
 
-        def term_by_term(terms, half, finish):
-            banks = []
-            for i in range(len(terms)):
-                a = terms[i][0]
-                if a not in quantised:
-                    quantise_activation(a)
-                    quantised.add(a)
-                last = i == len(terms) - 1
-                for rb in range(ROW_BLOCKS):
-                    if i == 0:
-                        banks.append(psum.tile([P, BANK], F32, name="sums", tag="bank"))
-                    multiply(banks[rb], terms[i], rb, half * BANK, BANK, first=(i == 0), last=last)
-                    if last:
-                        finish(banks[rb], rb, half * BANK, BANK)
+        def add_term(banks, term, half, first=False, finish=None):
+            for rb in range(ROW_BLOCKS):
+                multiply(banks[rb], term, rb, half * BANK, BANK, first=first, last=(finish is not None))
+                if finish is not None:
+                    finish(banks[rb], rb, half * BANK, BANK)
+
+        free_banks = list(HIGH_BANKS + LOW_BANKS)
 
         def bank_by_bank(terms, half, finish, widths, last_widths):
             for rb in range(ROW_BLOCKS):
                 column = half * BANK
                 for width in last_widths if rb == ROW_BLOCKS - 1 else widths:
-                    sums = psum.tile([P, width], F32, tag="bank")
+                    free_banks.append(free_banks.pop(0))
+                    sums = bank_tile(free_banks[-1], [P, width])
                     for i in range(len(terms)):
                         multiply(sums, terms[i], rb, column, width, first=(i == 0), last=(i == len(terms) - 1))
                     finish(sums, rb, column, width)
                     column += width
 
-        for half in range(HALVES):
-            term_by_term(CANDIDATE, half, finish_candidate)
-        for half in range(HALVES):
-            term_by_term(INPUT_GATE, half, finish_input_gate)
+        quantise_activation(X)
+        first_half = open_banks(HIGH_BANKS)
+        for first_rb in range(0, ROW_BLOCKS, ROWS_DMA):
+            for g in range(K_GROUPS):
+                for rb in range(first_rb, first_rb + ROWS_DMA):
+                    one_pass(first_half[rb], CANDIDATE[0], rb, g, 0, BANK, first=True, last=False)
+        quantise_activation(H)
+        second_half = open_banks(LOW_BANKS)
+        add_term(second_half, CANDIDATE[0], 1, first=True)
+        add_term(first_half, CANDIDATE[1], 0, finish=finish_candidate)
+        add_term(second_half, CANDIDATE[1], 1, finish=finish_candidate)
+        first_half = open_banks(HIGH_BANKS)
+        add_term(first_half, INPUT_GATE[0], 0, first=True)
+        add_term(first_half, INPUT_GATE[1], 0)
+        quantise_activation(C)
+        add_term(first_half, INPUT_GATE[2], 0, finish=finish_input_gate)
+        second_half = open_banks(LOW_BANKS)
+        add_term(second_half, INPUT_GATE[0], 1, first=True)
+        add_term(second_half, INPUT_GATE[1], 1)
+        add_term(second_half, INPUT_GATE[2], 1, finish=finish_input_gate)
         bank_by_bank(FORGET_GATE, 0, finish_forget_gate, (BANK,), (BANK,))
         bank_by_bank(FORGET_GATE, 1, finish_forget_gate, LATE_WIDTHS, LAST_WIDTHS)
         add_and_store()

@@ -129,7 +129,7 @@ def tile_lstm_peephole_build_pa_kernel(
                 )
 
         def load_scales(w):
-            for quadrant in range(QUADRANTS):
+            for quadrant in (0, 2, 1, 3):
                 nc.sync.dma_start(
                     out=w_scales[w][32 * quadrant : 32 * quadrant + 4 * K_GROUPS, :].bitcast(I32),
                     in_=weights[w][1][:, 4 * quadrant : 4 * quadrant + 4, :].bitcast(I32),

@@ -143,16 +143,20 @@ def tile_lstm_peephole_build_pa_kernel(
         load_scales(CANDIDATE[1][1])
         load_codes(CANDIDATE[1][1], 0)
         load_codes(CANDIDATE[1][1], 1)
-        rows_loaded = set((X, H))
-        for terms in (INPUT_GATE, FORGET_GATE):
-            for half in range(HALVES):
-                for a, w in terms:
-                    if a not in rows_loaded:
-                        load_rows(a)
-                        rows_loaded.add(a)
-                    if half == 0:
-                        load_scales(w)
-                    load_codes(w, half)
+        for a, w in INPUT_GATE[0:2]:
+            load_scales(w)
+            load_codes(w, 0)
+        load_rows(C)
+        load_codes(INPUT_GATE[0][1], 1)
+        load_scales(INPUT_GATE[2][1])
+        load_codes(INPUT_GATE[2][1], 0)
+        load_codes(INPUT_GATE[1][1], 1)
+        load_codes(INPUT_GATE[2][1], 1)
+        for half in range(HALVES):
+            for a, w in FORGET_GATE:
+                if half == 0:
+                    load_scales(w)
+                load_codes(w, half)
 
         def quantise_activation(a):
             grouped_tiles = []
@@ -257,9 +261,9 @@ def tile_lstm_peephole_build_pa_kernel(
         add_term(first_half, INPUT_GATE[0], 0, first=True)
         add_term(first_half, INPUT_GATE[1], 0)
         quantise_activation(C)
-        add_term(first_half, INPUT_GATE[2], 0, finish=finish_input_gate)
         second_half = open_banks(LOW_BANKS)
         add_term(second_half, INPUT_GATE[0], 1, first=True)
+        add_term(first_half, INPUT_GATE[2], 0, finish=finish_input_gate)
         add_term(second_half, INPUT_GATE[1], 1)
         add_term(second_half, INPUT_GATE[2], 1, finish=finish_input_gate)
         bank_by_bank(FORGET_GATE, 0, finish_forget_gate, (BANK,), (BANK,))

from contextlib import ExitStack

import concourse.mybir as mybir
from concourse.masks import make_identity

FP8X4 = mybir.dt.float8_e4m3fn_x4
BF16 = mybir.dt.bfloat16
F32 = mybir.dt.float32
I32 = mybir.dt.int32
U32 = mybir.dt.uint32
U8 = mybir.dt.uint8
ACT = mybir.ActivationFunctionType

P = 128
PACK = 4
K_PASS = P * PACK
PAIR = 2
BANK = 512
PSUM_BANKS = 8
LOW_BANKS = (0, 1, 2, 3)
HIGH_BANKS = (4, 5, 6, 7)

BATCH = 512
K = 1024
N = 1024
ROW_BLOCKS = BATCH // P
K_GROUPS = K // K_PASS
HALVES = N // BANK
WARM_MATMULS = 7
ROWS_DMA = 2
QUADRANTS = 4
LATE_WIDTHS = (256, 256)
LAST_WIDTHS = (256, 128, 128)

FLOPS = 8 * 2 * BATCH * K * N

X, H, C = 0, 1, 2
CANDIDATE = ((X, 0), (H, 1))
INPUT_GATE = ((X, 2), (H, 3), (C, 4))
FORGET_GATE = ((X, 5), (H, 6), (C, 7))


def tile_lstm_peephole_build_pa_kernel(
    tc,
    input_data,
    previous_hidden_state,
    previous_c_state,
    w_forget_words,
    w_forget_scales,
    w_input_words,
    w_input_scales,
    w_c_dash_words,
    w_c_dash_scales,
    w_forget_c_words,
    w_forget_c_scales,
    w_input_c_words,
    w_input_c_scales,
    w_ip_f_words,
    w_ip_f_scales,
    w_ip_i_words,
    w_ip_i_scales,
    w_ip_c_dash_words,
    w_ip_c_dash_scales,
    out,
):
    nc = tc.nc
    activations = (input_data, previous_hidden_state, previous_c_state)
    weights = (
        (w_ip_c_dash_words, w_ip_c_dash_scales),
        (w_c_dash_words, w_c_dash_scales),
        (w_ip_i_words, w_ip_i_scales),
        (w_input_words, w_input_scales),
        (w_input_c_words, w_input_c_scales),
        (w_ip_f_words, w_ip_f_scales),
        (w_forget_words, w_forget_scales),
        (w_forget_c_words, w_forget_c_scales),
    )

    with ExitStack() as ctx:
        keep = ctx.enter_context(tc.tile_pool(name="keep", bufs=1))
        stage = ctx.enter_context(tc.tile_pool(name="stage", bufs=ROW_BLOCKS))
        work = ctx.enter_context(tc.tile_pool(name="work", bufs=2 * ROW_BLOCKS))
        psum = ctx.enter_context(tc.psum_pool(name="psum", bufs=1))
        ctx.enter_context(tc.manual_schedule())

        def bank_tile(index, shape):
            return psum.tile(shape, F32, name="bank%d" % index, tag="bank%d" % index)

        identity = keep.tile([P, P], F32)
        table_warmer = keep.tile([P, 1], F32)
        rows = [keep.tile([P, ROW_BLOCKS, K], BF16, name="rows%d" % a) for a in range(3)]
        act_codes = [
            keep.tile([P, ROW_BLOCKS, K_GROUPS * P], U32, name="act_codes%d" % a, align_bytes=64) for a in range(3)
        ]
        act_scales = [
            keep.tile([P, ROW_BLOCKS, K_GROUPS * P], U8, name="act_scales%d" % a, align_bytes=64) for a in range(3)
        ]
        w_codes = [
            keep.tile([P, HALVES, K_GROUPS, BANK], U32, name="w_codes%d" % w, align_bytes=64)
            for w in range(len(weights))
        ]
        w_scales = [keep.tile([P, N], U8, name="w_scales%d" % w, align_bytes=64) for w in range(len(weights))]
        new_part = keep.tile([P, ROW_BLOCKS, N], F32)

        warm_zeros = keep.tile([P, BANK], BF16)
        nc.vector.memset(warm_zeros[:], 0.0)
        warm_bank = bank_tile(HIGH_BANKS[0], [P, BANK])
        for i in range(WARM_MATMULS):
            nc.tensor.matmul(out=warm_bank[:], lhsT=warm_zeros[:, 0:P], rhs=warm_zeros[:], start=True, stop=True)
        make_identity(nc, identity[:])
        nc.vector.memset(table_warmer[:], 0.0)
        nc.scalar.activation(out=table_warmer[:], in_=table_warmer[:], func=ACT.Sigmoid)
        for w in range(len(weights)):
            nc.vector.memset(w_scales[w][:].bitcast(I32), 0)

        def load_rows(a):
            for first in range(0, ROW_BLOCKS, ROWS_DMA):
                nc.sync.dma_start(
                    out=rows[a][:, first : first + ROWS_DMA, :],
                    in_=activations[a][first * P : (first + ROWS_DMA) * P, :].rearrange("(b p) k -> p b k", p=P),
                )

        def load_codes(w, half, groups_dma=K_GROUPS):
            source = weights[w][0].rearrange("g p n t -> p g (n t)")
            for g in range(0, K_GROUPS, groups_dma):
                nc.sync.dma_start(
                    out=w_codes[w][:, half, g : g + groups_dma, :].bitcast(I32),
                    in_=source[:, g : g + groups_dma, half * BANK * PACK : (half + 1) * BANK * PACK].bitcast(I32),
                )

        def load_scales(w):
            for quadrant in (0, 2, 1, 3):
                nc.sync.dma_start(
                    out=w_scales[w][32 * quadrant : 32 * quadrant + 4 * K_GROUPS, :].bitcast(I32),
                    in_=weights[w][1][:, 4 * quadrant : 4 * quadrant + 4, :].bitcast(I32),
                )

        load_rows(X)
        load_scales(CANDIDATE[0][1])
        load_codes(CANDIDATE[0][1], 0, groups_dma=1)
        load_rows(H)
        load_codes(CANDIDATE[0][1], 1)
        load_scales(CANDIDATE[1][1])
        load_codes(CANDIDATE[1][1], 0)
        load_codes(CANDIDATE[1][1], 1)
        for a, w in INPUT_GATE[0:2]:
            load_scales(w)
            load_codes(w, 0)
        load_rows(C)
        load_codes(INPUT_GATE[0][1], 1)
        load_scales(INPUT_GATE[2][1])
        load_codes(INPUT_GATE[2][1], 0)
        load_codes(INPUT_GATE[1][1], 1)
        load_codes(INPUT_GATE[2][1], 1)
        for half in range(HALVES):
            for a, w in FORGET_GATE:
                if half == 0:
                    load_scales(w)
                load_codes(w, half)

        def quantise_activation(a):
            grouped_tiles = []
            for rb in range(ROW_BLOCKS):
                words = rows[a][:, rb, :].bitcast(F32)
                sorted_words = stage.tile([P, K_GROUPS, PAIR, P], F32)
                nc.vector.tensor_copy(
                    out=sorted_words[:], in_=words.rearrange("r (g p u) -> r g u p", g=K_GROUPS, u=PAIR)
                )
                turned = bank_tile(LOW_BANKS[rb], [P, K_GROUPS, PAIR, P])
                for g in range(K_GROUPS):
                    for u in range(PAIR):
                        nc.tensor.transpose(turned[:, g, u, :], sorted_words[:, g, u, :], identity[:])
                grouped = stage.tile([P, K_GROUPS * P * PACK], BF16, align_bytes=64)
                nc.scalar.copy(
                    out=grouped[:].bitcast(F32).rearrange("p (g r u) -> p g r u", g=K_GROUPS, u=PAIR),
                    in_=turned[:].rearrange("p g u r -> p g r u"),
                )
                grouped_tiles.append(grouped)
            for rb in range(ROW_BLOCKS):
                nc.vector.quantize_mx(
                    out=act_codes[a][:, rb, :].bitcast(FP8X4),
                    scales=act_scales[a][:, rb, :],
                    in_=grouped_tiles[rb][:],
                )

        def one_pass(bank, term, rb, g, column, width, first, last):
            a, w = term
            half, inner = divmod(column, BANK)
            nc.tensor.matmul_mx(
                out=bank[:],
                lhsT=act_codes[a][:, rb, g * P : (g + 1) * P].bitcast(FP8X4),
                lhsT_scale=act_scales[a][:, rb, g * P : (g + 1) * P],
                rhs=w_codes[w][:, half, g, inner : inner + width].bitcast(FP8X4),
                rhs_scale=w_scales[w][4 * g : P, column : column + width],
                start=(first and g == 0),
                stop=(last and g == K_GROUPS - 1),
            )

        def multiply(bank, term, rb, column, width, first, last):
            for g in range(K_GROUPS):
                one_pass(bank, term, rb, g, column, width, first, last)

        def finish_candidate(bank, rb, column, width):
            nc.scalar.activation(out=new_part[:, rb, column : column + width], in_=bank[:], func=ACT.Tanh)

        def finish_input_gate(bank, rb, column, width):
            gate = work.tile([P, width], F32)
            nc.scalar.activation(out=gate[:], in_=bank[:], func=ACT.Sigmoid)
            product = new_part[:, rb, column : column + width]
            nc.vector.tensor_mul(out=product, in0=gate[:], in1=product)

        waiting_sums = []

        def add_and_store():
            gate, rb, column, width = waiting_sums.pop(0)
            nc.vector.tensor_add(out=gate[:], in0=gate[:], in1=new_part[:, rb, column : column + width])
            nc.sync.dma_start(out=out[rb * P : (rb + 1) * P, column : column + width], in_=gate[:])

        def finish_forget_gate(bank, rb, column, width):
            gate = work.tile([P, width], F32)
            nc.scalar.activation(out=gate[:], in_=bank[:], func=ACT.Sigmoid)
            nc.vector.tensor_mul(out=gate[:], in0=gate[:], in1=rows[C][:, rb, column : column + width])
            waiting_sums.append((gate, rb, column, width))
            if len(waiting_sums) > 1:
                add_and_store()

        def open_banks(indices):
            return [bank_tile(index, [P, BANK]) for index in indices]

        def add_term(banks, term, half, first=False, finish=None):
            for rb in range(ROW_BLOCKS):
                multiply(banks[rb], term, rb, half * BANK, BANK, first=first, last=(finish is not None))
                if finish is not None:
                    finish(banks[rb], rb, half * BANK, BANK)

        free_banks = list(HIGH_BANKS + LOW_BANKS)

        def bank_by_bank(terms, half, finish, widths, last_widths):
            for rb in range(ROW_BLOCKS):
                column = half * BANK
                for width in last_widths if rb == ROW_BLOCKS - 1 else widths:
                    free_banks.append(free_banks.pop(0))
                    sums = bank_tile(free_banks[-1], [P, width])
                    for i in range(len(terms)):
                        multiply(sums, terms[i], rb, column, width, first=(i == 0), last=(i == len(terms) - 1))
                    finish(sums, rb, column, width)
                    column += width

        quantise_activation(X)
        first_half = open_banks(HIGH_BANKS)
        for first_rb in range(0, ROW_BLOCKS, ROWS_DMA):
            for g in range(K_GROUPS):
                for rb in range(first_rb, first_rb + ROWS_DMA):
                    one_pass(first_half[rb], CANDIDATE[0], rb, g, 0, BANK, first=True, last=False)
        quantise_activation(H)
        second_half = open_banks(LOW_BANKS)
        add_term(second_half, CANDIDATE[0], 1, first=True)
        add_term(first_half, CANDIDATE[1], 0, finish=finish_candidate)
        add_term(second_half, CANDIDATE[1], 1, finish=finish_candidate)
        first_half = open_banks(HIGH_BANKS)
        add_term(first_half, INPUT_GATE[0], 0, first=True)
        add_term(first_half, INPUT_GATE[1], 0)
        quantise_activation(C)
        second_half = open_banks(LOW_BANKS)
        add_term(second_half, INPUT_GATE[0], 1, first=True)
        add_term(first_half, INPUT_GATE[2], 0, finish=finish_input_gate)
        add_term(second_half, INPUT_GATE[1], 1)
        add_term(second_half, INPUT_GATE[2], 1, finish=finish_input_gate)
        bank_by_bank(FORGET_GATE, 0, finish_forget_gate, (BANK,), (BANK,))
        bank_by_bank(FORGET_GATE, 1, finish_forget_gate, LATE_WIDTHS, LAST_WIDTHS)
        add_and_store()
